import numpy as np
import ml_dtypes


def mxq(x, axis, fmt="e4m3"):
    dtype, down = {"e4m3": (ml_dtypes.float8_e4m3fn, 7), "e5m2": (ml_dtypes.float8_e5m2, 14)}[fmt]
    v = np.moveaxis(np.asarray(x, np.float32).astype(ml_dtypes.bfloat16).astype(np.float64), axis, -1)
    blocks = v.reshape(v.shape[:-1] + (-1, 32))
    amax = np.abs(blocks).max(-1, keepdims=True)
    byte = np.maximum(np.where(amax > 0, np.frexp(amax)[1] - 1 + 127, 0) - down, 1)
    scale = np.exp2(byte - 127.0)
    codes = (blocks / scale).astype(np.float32).astype(dtype).astype(np.float64)
    return np.moveaxis((codes * scale).reshape(v.shape), -1, axis)


WIDE = False


def mx_kscale(k):
    if not WIDE:
        return np.ones(k)
    levels = np.array([10, -10, 5, -5, 0])
    a = np.random.permutation(np.resize(levels, k // 512 * 4)).reshape(k // 512, 4)
    idx = np.arange(k)
    return np.exp2(a[idx // 512, idx % 128 // 32])


BF16 = ml_dtypes.bfloat16


def bf(x):
    return np.asarray(x, np.float32).astype(BF16)


def f64(x):
    return np.asarray(x).astype(np.float64)


E2M1 = np.array([0.0, 0.5, 1.0, 1.5, 2.0, 3.0, 4.0, 6.0, -0.0, -0.5, -1.0, -1.5, -2.0, -3.0, -4.0, -6.0])


def pack_weight(w, fmt):
    k, n = w.shape
    w = f64(bf(w)).reshape(k // 32, 32, n)
    amax = np.abs(w).max(1)
    if fmt == "e4m3":
        byte = np.frexp(amax)[1] - 1 + 127 - 7
    else:
        mant, ex = np.frexp(amax / 6.0)
        byte = np.where(mant > 0.5, ex, ex - 1) + 127
    byte = np.clip(np.where(amax > 0, byte, 1), 1, 254)
    scaled = (w * np.exp2(127.0 - byte)[:, None, :]).reshape(k, n).astype(np.float32)
    by_word = np.ascontiguousarray(scaled.reshape(k // 512, 128, 4, n).transpose(0, 1, 3, 2))
    if fmt == "e4m3":
        words = by_word.astype(ml_dtypes.float8_e4m3fn).view(np.uint8)
    else:
        c = by_word.astype(ml_dtypes.float4_e2m1fn).view(np.uint8) & 0xF
        words = c[..., 0::2] | (c[..., 1::2] << 4)
    return np.ascontiguousarray(words), np.ascontiguousarray(byte.astype(np.uint8).reshape(k // 512, 16, n))


def unpack_weight(words, scales, fmt):
    g, p, n, _ = words.shape
    if fmt == "e4m3":
        vals = np.ascontiguousarray(words).view(ml_dtypes.float8_e4m3fn).astype(np.float64)
    else:
        nib = np.empty((g, p, n, 4), np.uint8)
        nib[..., 0::2] = words & 0xF
        nib[..., 1::2] = words >> 4
        vals = E2M1[nib]
    vals = vals * np.repeat(np.exp2(scales.astype(np.float64) - 127.0), 8, axis=1)[..., None]
    return vals.transpose(0, 1, 3, 2).reshape(g * 512, n)


B, IN, OUT, POOL_K = 128, 4096, 4096, 4
SCALE = 2.0
FMT = "e4m3"


def _gelu_tanh(p):
    return 0.5 * p * (1.0 + np.tanh(0.7978845608 * (p + 0.044715 * p * p * p)))


def setup_inputs():
    s = mx_kscale(IN)
    x = bf(np.random.standard_normal((B, IN)) * s)
    weight = np.random.standard_normal((OUT, IN)) * (1.0 / np.sqrt(IN)) / s[None, :]
    words, scales = pack_weight(np.ascontiguousarray(weight.T), FMT)
    bias = bf(np.random.standard_normal(OUT) * 0.5)
    return {"x": x,
            "weight_words": words,
            "weight_scales": scales,
            "bias": bias}


def reference(x, weight_words, weight_scales, bias):
    w = unpack_weight(weight_words, weight_scales, FMT)
    rows = x.shape[0]
    width = w.shape[1]
    y = (mxq(f64(x), 1, "e4m3") @ w) + f64(bias)
    pooled = y.reshape(rows, width // POOL_K, POOL_K).mean(axis=-1)
    scaled = _gelu_tanh(pooled) * SCALE
    return np.max(scaled, axis=1)

@@ -1,0 +1,180 @@
+from contextlib import ExitStack
+
+import concourse.mybir as mybir
+from concourse.masks import make_identity
+
+F32 = mybir.dt.float32
+BF16 = mybir.dt.bfloat16
+I32 = mybir.dt.int32
+U32 = mybir.dt.uint32
+U8 = mybir.dt.uint8
+FP8X4 = mybir.dt.float8_e4m3fn_x4
+ADD = mybir.AluOpType.add
+MAX = mybir.AluOpType.max
+AXIS_X = mybir.AxisListType.X
+GELU = mybir.ActivationFunctionType.Gelu_apprx_tanh
+
+P = 128
+B = 128
+IN = 4096
+OUT = 4096
+POOL_K = 4
+K_PASS = 512
+GROUPS = IN // K_PASS
+N_TILE = 512
+BANKS = OUT // N_TILE
+J_TILE = N_TILE // POOL_K
+WHOLE_GROUPS = 6
+
+FLOPS = 2 * B * IN * OUT
+
+
+def tile_modelnew_w_kernel(tc, x, weight_words, weight_scales, bias, out):
+    nc = tc.nc
+    with ExitStack() as ctx:
+        ctx.enter_context(tc.manual_schedule())
+        keep = ctx.enter_context(tc.tile_pool(name="keep", bufs=1))
+        psum = ctx.enter_context(tc.psum_pool(name="psum", bufs=1))
+
+        ww = weight_words.bitcast(I32).rearrange("g p n o -> p g (n o)")
+
+        x_sb = keep.tile([P, IN], BF16, name="x_sb")
+        nc.sync.dma_start(out=x_sb[:], in_=x)
+        bias_sb = keep.tile([P, 2, 16], BF16, name="bias_sb")
+        nc.scalar.dma_start(out=bias_sb[:], in_=bias.rearrange("(h p e) -> p h e", h=2, e=16))
+
+        planes = keep.tile([P, 2, OUT], U8, name="planes", align_bytes=64)
+        nc.vector.memset(planes[:].rearrange("p h n -> p (h n)").bitcast(I32), 0)
+        warm = keep.tile([P, 1], F32, name="warm")
+        nc.vector.memset(warm[:], 0.0)
+        warm_out = keep.tile([P, 1], F32, name="warm_out")
+        nc.scalar.activation(out=warm_out[:], in_=warm[:], func=GELU)
+
+        ident = keep.tile([P, P], F32, name="ident")
+        make_identity(nc, ident[:])
+
+        for h in range(2):
+            for q in range(4):
+                nc.gpsimd.dma_start(
+                    out=planes[32 * q : 32 * q + 16, h, :].bitcast(F32),
+                    in_=weight_scales[4 * h : 4 * h + 4, 4 * q : 4 * q + 4, :].bitcast(F32),
+                )
+
+        w_whole = []
+        for g in range(WHOLE_GROUPS):
+            w_g = keep.tile([P, OUT], I32, name="w%d" % g, align_bytes=64)
+            nc.sync.dma_start(out=w_g[:], in_=ww[:, g, :])
+            w_whole.append(w_g)
+        w_late = []
+        for t in range(BANKS):
+            cols = slice(N_TILE * t, N_TILE * (t + 1))
+            w_t = keep.tile([P, GROUPS - WHOLE_GROUPS, N_TILE], I32, name="wl%d" % t, align_bytes=64)
+            if t < BANKS - 1:
+                nc.sync.dma_start(out=w_t[:], in_=ww[:, WHOLE_GROUPS:GROUPS, cols])
+            else:
+                for gi in range(GROUPS - WHOLE_GROUPS):
+                    nc.sync.dma_start(out=w_t[:, gi, :], in_=ww[:, WHOLE_GROUPS + gi, cols])
+            w_late.append(w_t)
+
+        x_words = x_sb[:].bitcast(F32)
+        grouped = keep.tile([P, IN], BF16, name="grouped", align_bytes=64)
+        grouped_words = grouped[:].bitcast(F32).rearrange("p (g b u) -> p g b u", g=GROUPS, u=2)
+        x_codes = keep.tile([P, GROUPS * B], U32, name="x_codes", align_bytes=64)
+        x_scales = keep.tile([P, GROUPS * B], U8, name="x_scales", align_bytes=64)
+        xts = []
+        for i in range(4):
+            xt = psum.tile([P, 2, 2, B], F32, name="xt%d" % i, tag="bank%d" % i)
+            for gl in range(2):
+                g = 2 * i + gl
+                for u in range(2):
+                    nc.tensor.transpose(xt[:, gl, u, :], x_words[:, 256 * g + u : 256 * (g + 1) : 2], ident[:])
+            xts.append(xt)
+
+        bias_pool = keep.tile([P, 8], F32, name="bias_pool")
+        nc.vector.tensor_reduce(
+            out=bias_pool[:],
+            in_=bias_sb[:].rearrange("p h (c i) -> p (h c) i", i=POOL_K),
+            axis=AXIS_X,
+            op=ADD,
+        )
+        bts = []
+        for h in range(2):
+            bt = psum.tile([P, 4, P], F32, name="bt%d" % h, tag="bank%d" % (4 + h))
+            for c in range(4):
+                nc.tensor.transpose(
+                    bt[:, c, :], bias_pool[:, 4 * h + c : 4 * h + c + 1].to_broadcast([P, P]), ident[:]
+                )
+            bts.append(bt)
+
+        for i in (0, 2):
+            nc.vector.tensor_copy(
+                out=grouped_words[:, 2 * i : 2 * i + 2, :, :], in_=xts[i][:].rearrange("p g u b -> p g b u")
+            )
+            nc.scalar.copy(
+                out=grouped_words[:, 2 * i + 2 : 2 * i + 4, :, :],
+                in_=xts[i + 1][:].rearrange("p g u b -> p g b u"),
+            )
+        for half in range(2):
+            nc.vector.quantize_mx(
+                out=x_codes[:, 512 * half : 512 * (half + 1)].bitcast(FP8X4),
+                scales=x_scales[:, 512 * half : 512 * (half + 1)],
+                in_=grouped[:, 2048 * half : 2048 * (half + 1)],
+            )
+        bias_all = keep.tile([P, OUT // POOL_K], F32, name="bias_all")
+        for h in range(2):
+            nc.scalar.copy(
+                out=bias_all[:, 512 * h : 512 * (h + 1)].rearrange("p (n c) -> p n c", c=4),
+                in_=bts[h][:].rearrange("p c n -> p n c"),
+            )
+
+        def mx_pass(acc, g, t, rhs):
+            k = 4 * (g % 4)
+            nc.tensor.matmul_mx(
+                out=acc[:],
+                lhsT=x_codes[:, B * g : B * (g + 1)].bitcast(FP8X4),
+                lhsT_scale=x_scales[:, B * g : B * (g + 1)],
+                rhs=rhs.bitcast(FP8X4),
+                rhs_scale=planes[k:P, g // 4, N_TILE * t : N_TILE * (t + 1)],
+                start=(g == 0),
+                stop=(g == GROUPS - 1),
+            )
+
+        accs = []
+        for t in range(BANKS):
+            acc = psum.tile([P, N_TILE], F32, name="acc%d" % t, tag="bank%d" % t)
+            accs.append(acc)
+        for g in range(WHOLE_GROUPS):
+            for t in range(BANKS):
+                mx_pass(accs[t], g, t, w_whole[g][:, N_TILE * t : N_TILE * (t + 1)])
+
+        last = keep.tile([P, J_TILE + 8], F32, name="last")
+        gelus = []
+        for t in range(BANKS):
+            for gi in range(GROUPS - WHOLE_GROUPS):
+                mx_pass(accs[t], WHOLE_GROUPS + gi, t, w_late[t][:, gi, :])
+            pooled = keep.tile([P, J_TILE], F32, name="pooled%d" % t)
+            nc.vector.tensor_reduce(
+                out=pooled[:], in_=accs[t][:].rearrange("p (j i) -> p j i", i=POOL_K), axis=AXIS_X, op=ADD
+            )
+            biased = keep.tile([P, J_TILE], F32, name="biased%d" % t)
+            nc.vector.tensor_tensor(
+                out=biased[:], in0=pooled[:], in1=bias_all[:, J_TILE * t : J_TILE * (t + 1)], op=ADD
+            )
+            if t < BANKS - 1:
+                gelu = keep.tile([P, J_TILE], F32, name="gelu%d" % t)
+                nc.scalar.activation(out=gelu[:], in_=biased[:], func=GELU, scale=1.0 / POOL_K)
+                gelus.append(gelu)
+            else:
+                nc.scalar.activation(out=last[:, 0:J_TILE], in_=biased[:], func=GELU, scale=1.0 / POOL_K)
+            if t > 0:
+                nc.vector.tensor_reduce(
+                    out=last[:, J_TILE + t - 1 : J_TILE + t], in_=gelus[t - 1][:], axis=AXIS_X, op=MAX
+                )
+
+        best = keep.tile([P, 1], F32, name="best")
+        nc.vector.tensor_reduce(out=best[:], in_=last[:, 0 : J_TILE + BANKS - 1], axis=AXIS_X, op=MAX)
+        fin = psum.tile([P, P], F32, name="fin", tag="bank0")
+        nc.tensor.transpose(fin[:], best[:, 0:1].to_broadcast([P, P]), ident[:])
+        res = keep.tile([P, P], F32, name="res")
+        nc.vector.tensor_scalar_mul(out=res[:], in0=fin[:], scalar1=2.0)
+        nc.sync.dma_start(out=out.rearrange("(o b) -> o b", o=1), in_=res[0:1, :])

@@ -43,8 +43,11 @@ def tile_modelnew_w_kernel(tc, x, weight_words, weight_scales, bias, out):
         bias_sb = keep.tile([P, 2, 16], BF16, name="bias_sb")
         nc.scalar.dma_start(out=bias_sb[:], in_=bias.rearrange("(h p e) -> p h e", h=2, e=16))
 
-        planes = keep.tile([P, 2, OUT], U8, name="planes", align_bytes=64)
-        nc.vector.memset(planes[:].rearrange("p h n -> p (h n)").bitcast(I32), 0)
+        planes = []
+        for h in range(2):
+            plane = keep.tile([P, OUT], U8, name="planes%d" % h, align_bytes=64)
+            nc.vector.memset(plane[:].bitcast(I32), 0)
+            planes.append(plane)
         warm = keep.tile([P, 1], F32, name="warm")
         nc.vector.memset(warm[:], 0.0)
         warm_out = keep.tile([P, 1], F32, name="warm_out")
@@ -55,9 +58,9 @@ def tile_modelnew_w_kernel(tc, x, weight_words, weight_scales, bias, out):
 
         for h in range(2):
             for q in range(4):
-                nc.gpsimd.dma_start(
-                    out=planes[32 * q : 32 * q + 16, h, :].bitcast(F32),
-                    in_=weight_scales[4 * h : 4 * h + 4, 4 * q : 4 * q + 4, :].bitcast(F32),
+                nc.sync.dma_start(
+                    out=planes[h][32 * q : 32 * q + 16, :].bitcast(I32),
+                    in_=weight_scales[4 * h : 4 * h + 4, 4 * q : 4 * q + 4, :].bitcast(I32),
                 )
 
         w_whole = []
@@ -134,7 +137,7 @@ def tile_modelnew_w_kernel(tc, x, weight_words, weight_scales, bias, out):
                 lhsT=x_codes[:, B * g : B * (g + 1)].bitcast(FP8X4),
                 lhsT_scale=x_scales[:, B * g : B * (g + 1)],
                 rhs=rhs.bitcast(FP8X4),
-                rhs_scale=planes[k:P, g // 4, N_TILE * t : N_TILE * (t + 1)],
+                rhs_scale=planes[g // 4][k:P, N_TILE * t : N_TILE * (t + 1)],
                 start=(g == 0),
                 stop=(g == GROUPS - 1),
             )

@@ -58,9 +58,9 @@ def tile_modelnew_w_kernel(tc, x, weight_words, weight_scales, bias, out):
 
         for h in range(2):
             for q in range(4):
-                nc.sync.dma_start(
-                    out=planes[h][32 * q : 32 * q + 16, :].bitcast(I32),
-                    in_=weight_scales[4 * h : 4 * h + 4, 4 * q : 4 * q + 4, :].bitcast(I32),
+                nc.gpsimd.dma_start(
+                    out=planes[h][32 * q : 32 * q + 16, :].bitcast(F32),
+                    in_=weight_scales[4 * h : 4 * h + 4, 4 * q : 4 * q + 4, :].bitcast(F32),
                 )
 
         w_whole = []

@@ -58,9 +58,9 @@ def tile_modelnew_w_kernel(tc, x, weight_words, weight_scales, bias, out):
 
         for h in range(2):
             for q in range(4):
-                nc.gpsimd.dma_start(
-                    out=planes[h][32 * q : 32 * q + 16, :].bitcast(F32),
-                    in_=weight_scales[4 * h : 4 * h + 4, 4 * q : 4 * q + 4, :].bitcast(F32),
+                nc.sync.dma_start(
+                    out=planes[h][32 * q : 32 * q + 16, :].bitcast(I32),
+                    in_=weight_scales[4 * h : 4 * h + 4, 4 * q : 4 * q + 4, :].bitcast(I32),
                 )
 
         w_whole = []
@@ -159,8 +159,13 @@ def tile_modelnew_w_kernel(tc, x, weight_words, weight_scales, bias, out):
             nc.vector.tensor_reduce(
                 out=pooled[:], in_=accs[t][:].rearrange("p (j i) -> p j i", i=POOL_K), axis=AXIS_X, op=ADD
             )
+            if t > 0:
+                nc.vector.tensor_reduce(
+                    out=last[:, J_TILE + t - 1 : J_TILE + t], in_=gelus[t - 1][:], axis=AXIS_X, op=MAX
+                )
             biased = keep.tile([P, J_TILE], F32, name="biased%d" % t)
-            nc.vector.tensor_tensor(
+            adder = nc.gpsimd if t < BANKS - 1 else nc.vector
+            adder.tensor_tensor(
                 out=biased[:], in0=pooled[:], in1=bias_all[:, J_TILE * t : J_TILE * (t + 1)], op=ADD
             )
             if t < BANKS - 1:
@@ -169,10 +174,6 @@ def tile_modelnew_w_kernel(tc, x, weight_words, weight_scales, bias, out):
                 gelus.append(gelu)
             else:
                 nc.scalar.activation(out=last[:, 0:J_TILE], in_=biased[:], func=GELU, scale=1.0 / POOL_K)
-            if t > 0:
-                nc.vector.tensor_reduce(
-                    out=last[:, J_TILE + t - 1 : J_TILE + t], in_=gelus[t - 1][:], axis=AXIS_X, op=MAX
-                )
 
         best = keep.tile([P, 1], F32, name="best")
         nc.vector.tensor_reduce(out=best[:], in_=last[:, 0 : J_TILE + BANKS - 1], axis=AXIS_X, op=MAX)

@@ -146,37 +146,45 @@ def tile_modelnew_w_kernel(tc, x, weight_words, weight_scales, bias, out):
         for t in range(BANKS):
             acc = psum.tile([P, N_TILE], F32, name="acc%d" % t, tag="bank%d" % t)
             accs.append(acc)
-        for g in range(WHOLE_GROUPS):
+        for g in range(WHOLE_GROUPS - 1):
             for t in range(BANKS):
                 mx_pass(accs[t], g, t, w_whole[g][:, N_TILE * t : N_TILE * (t + 1)])
 
         last = keep.tile([P, J_TILE + 8], F32, name="last")
-        gelus = []
+        gelus = keep.tile([P, BANKS - 1, J_TILE], F32, name="gelus")
+
+        def bank_max(t0, t1):
+            nc.vector.tensor_reduce(
+                out=last[:, J_TILE + t0 : J_TILE + t0 + 1],
+                in_=gelus[:, t0:t1, :].rearrange("p t j -> p (t j)"),
+                axis=AXIS_X,
+                op=MAX,
+            )
+
         for t in range(BANKS):
+            g = WHOLE_GROUPS - 1
+            mx_pass(accs[t], g, t, w_whole[g][:, N_TILE * t : N_TILE * (t + 1)])
             for gi in range(GROUPS - WHOLE_GROUPS):
                 mx_pass(accs[t], WHOLE_GROUPS + gi, t, w_late[t][:, gi, :])
             pooled = keep.tile([P, J_TILE], F32, name="pooled%d" % t)
             nc.vector.tensor_reduce(
                 out=pooled[:], in_=accs[t][:].rearrange("p (j i) -> p j i", i=POOL_K), axis=AXIS_X, op=ADD
             )
-            if t > 0:
-                nc.vector.tensor_reduce(
-                    out=last[:, J_TILE + t - 1 : J_TILE + t], in_=gelus[t - 1][:], axis=AXIS_X, op=MAX
-                )
             biased = keep.tile([P, J_TILE], F32, name="biased%d" % t)
+            if 2 <= t < BANKS - 1:
+                bank_max(t - 2, t - 1)
             adder = nc.gpsimd if t < BANKS - 1 else nc.vector
             adder.tensor_tensor(
                 out=biased[:], in0=pooled[:], in1=bias_all[:, J_TILE * t : J_TILE * (t + 1)], op=ADD
             )
             if t < BANKS - 1:
-                gelu = keep.tile([P, J_TILE], F32, name="gelu%d" % t)
-                nc.scalar.activation(out=gelu[:], in_=biased[:], func=GELU, scale=1.0 / POOL_K)
-                gelus.append(gelu)
+                nc.scalar.activation(out=gelus[:, t, :], in_=biased[:], func=GELU, scale=1.0 / POOL_K)
             else:
                 nc.scalar.activation(out=last[:, 0:J_TILE], in_=biased[:], func=GELU, scale=1.0 / POOL_K)
+                bank_max(BANKS - 3, BANKS - 1)
 
         best = keep.tile([P, 1], F32, name="best")
-        nc.vector.tensor_reduce(out=best[:], in_=last[:, 0 : J_TILE + BANKS - 1], axis=AXIS_X, op=MAX)
+        nc.vector.tensor_reduce(out=best[:], in_=last[:, 0 : J_TILE + BANKS - 2], axis=AXIS_X, op=MAX)
         fin = psum.tile([P, P], F32, name="fin", tag="bank0")
         nc.tensor.transpose(fin[:], best[:, 0:1].to_broadcast([P, P]), ident[:])
         res = keep.tile([P, P], F32, name="res")

@@ -57,10 +57,11 @@ def tile_modelnew_w_kernel(tc, x, weight_words, weight_scales, bias, out):
         make_identity(nc, ident[:])
 
         for h in range(2):
+            queue, view = (nc.sync, I32) if h == 0 else (nc.gpsimd, F32)
             for q in range(4):
-                nc.sync.dma_start(
-                    out=planes[h][32 * q : 32 * q + 16, :].bitcast(I32),
-                    in_=weight_scales[4 * h : 4 * h + 4, 4 * q : 4 * q + 4, :].bitcast(I32),
+                queue.dma_start(
+                    out=planes[h][32 * q : 32 * q + 16, :].bitcast(view),
+                    in_=weight_scales[4 * h : 4 * h + 4, 4 * q : 4 * q + 4, :].bitcast(view),
                 )
 
         w_whole = []

@@ -11,6 +11,7 @@ U8 = mybir.dt.uint8
 FP8X4 = mybir.dt.float8_e4m3fn_x4
 ADD = mybir.AluOpType.add
 MAX = mybir.AluOpType.max
+MULT = mybir.AluOpType.mult
 AXIS_X = mybir.AxisListType.X
 GELU = mybir.ActivationFunctionType.Gelu_apprx_tanh
 
@@ -48,6 +49,8 @@ def tile_modelnew_w_kernel(tc, x, weight_words, weight_scales, bias, out):
             plane = keep.tile([P, OUT], U8, name="planes%d" % h, align_bytes=64)
             nc.vector.memset(plane[:].bitcast(I32), 0)
             planes.append(plane)
+        best = keep.tile([P, 32], F32, name="best", align_bytes=64)
+        nc.vector.memset(best[:], 0.0)
         warm = keep.tile([P, 1], F32, name="warm")
         nc.vector.memset(warm[:], 0.0)
         warm_out = keep.tile([P, 1], F32, name="warm_out")
@@ -184,10 +187,16 @@ def tile_modelnew_w_kernel(tc, x, weight_words, weight_scales, bias, out):
                 nc.scalar.activation(out=last[:, 0:J_TILE], in_=biased[:], func=GELU, scale=1.0 / POOL_K)
                 bank_max(BANKS - 3, BANKS - 1)
 
-        best = keep.tile([P, 1], F32, name="best")
-        nc.vector.tensor_reduce(out=best[:], in_=last[:, 0 : J_TILE + BANKS - 2], axis=AXIS_X, op=MAX)
-        fin = psum.tile([P, P], F32, name="fin", tag="bank0")
-        nc.tensor.transpose(fin[:], best[:, 0:1].to_broadcast([P, P]), ident[:])
-        res = keep.tile([P, P], F32, name="res")
-        nc.vector.tensor_scalar_mul(out=res[:], in0=fin[:], scalar1=2.0)
-        nc.sync.dma_start(out=out.rearrange("(o b) -> o b", o=1), in_=res[0:1, :])
+        doubled = keep.tile([P, J_TILE + 8], F32, name="doubled")
+        nc.vector.tensor_scalar(
+            out=doubled[:, 0 : J_TILE + BANKS - 2],
+            in0=last[:, 0 : J_TILE + BANKS - 2],
+            scalar1=2.0,
+            scalar2=None,
+            op0=MULT,
+            op1=MAX,
+            accum_out=best[:, 0:1],
+        )
+        rows = keep.tile([P, 32], F32, name="rows", align_bytes=64)
+        nc.vector.transpose(out=rows[:], in_=best[:])
+        nc.sync.dma_start(out=out.rearrange("(q b) -> q b", q=4), in_=rows[0:P:32, :])

@@ -60,8 +60,8 @@ def tile_modelnew_w_kernel(tc, x, weight_words, weight_scales, bias, out):
         make_identity(nc, ident[:])
 
         for h in range(2):
-            queue, view = (nc.sync, I32) if h == 0 else (nc.gpsimd, F32)
             for q in range(4):
+                queue, view = (nc.sync, I32) if q < 2 else (nc.gpsimd, F32)
                 queue.dma_start(
                     out=planes[h][32 * q : 32 * q + 16, :].bitcast(view),
                     in_=weight_scales[4 * h : 4 * h + 4, 4 * q : 4 * q + 4, :].bitcast(view),

@@ -41,8 +41,8 @@ def tile_modelnew_w_kernel(tc, x, weight_words, weight_scales, bias, out):
 
         x_sb = keep.tile([P, IN], BF16, name="x_sb")
         nc.sync.dma_start(out=x_sb[:], in_=x)
-        bias_sb = keep.tile([P, 2, 16], BF16, name="bias_sb")
-        nc.scalar.dma_start(out=bias_sb[:], in_=bias.rearrange("(h p e) -> p h e", h=2, e=16))
+        bias_rows = keep.tile([P, N_TILE], BF16, name="bias_rows")
+        nc.scalar.dma_start(out=bias_rows[0:BANKS, :], in_=bias.rearrange("(t n) -> t n", t=BANKS))
 
         planes = []
         for h in range(2):
@@ -97,10 +97,11 @@ def tile_modelnew_w_kernel(tc, x, weight_words, weight_scales, bias, out):
                     nc.tensor.transpose(xt[:, gl, u, :], x_words[:, 256 * g + u : 256 * (g + 1) : 2], ident[:])
             xts.append(xt)
 
-        bias_pool = keep.tile([P, 8], F32, name="bias_pool")
+        bias_pool = keep.tile([P, J_TILE], F32, name="bias_pool")
+        nc.vector.memset(bias_pool[:], 0.0)
         nc.vector.tensor_reduce(
-            out=bias_pool[:],
-            in_=bias_sb[:].rearrange("p h (c i) -> p (h c) i", i=POOL_K),
+            out=bias_pool[0:BANKS, :],
+            in_=bias_rows[0:BANKS, :].rearrange("p (j i) -> p j i", i=POOL_K),
             axis=AXIS_X,
             op=ADD,
         )
@@ -108,8 +109,12 @@ def tile_modelnew_w_kernel(tc, x, weight_words, weight_scales, bias, out):
         for h in range(2):
             bt = psum.tile([P, 4, P], F32, name="bt%d" % h, tag="bank%d" % (4 + h))
             for c in range(4):
-                nc.tensor.transpose(
-                    bt[:, c, :], bias_pool[:, 4 * h + c : 4 * h + c + 1].to_broadcast([P, P]), ident[:]
+                nc.tensor.matmul(
+                    out=bt[:, c, :],
+                    lhsT=ident[:, 4 * h + c : 4 * h + c + 1].to_broadcast([P, P]),
+                    rhs=bias_pool[:],
+                    start=True,
+                    stop=True,
                 )
             bts.append(bt)
 
@@ -129,10 +134,7 @@ def tile_modelnew_w_kernel(tc, x, weight_words, weight_scales, bias, out):
             )
         bias_all = keep.tile([P, OUT // POOL_K], F32, name="bias_all")
         for h in range(2):
-            nc.scalar.copy(
-                out=bias_all[:, 512 * h : 512 * (h + 1)].rearrange("p (n c) -> p n c", c=4),
-                in_=bts[h][:].rearrange("p c n -> p n c"),
-            )
+            nc.scalar.copy(out=bias_all[:, 512 * h : 512 * (h + 1)], in_=bts[h][:].rearrange("p c n -> p (c n)"))
 
         def mx_pass(acc, g, t, rhs):
             k = 4 * (g % 4)

@@ -25,7 +25,10 @@ GROUPS = IN // K_PASS
 N_TILE = 512
 BANKS = OUT // N_TILE
 J_TILE = N_TILE // POOL_K
-WHOLE_GROUPS = 6
+WHOLE_GROUPS = 2
+A_BANKS = 6
+A_COLS = A_BANKS * N_TILE
+LATE_FROM = 6
 
 FLOPS = 2 * B * IN * OUT
 
@@ -72,15 +75,25 @@ def tile_modelnew_w_kernel(tc, x, weight_words, weight_scales, bias, out):
             w_g = keep.tile([P, OUT], I32, name="w%d" % g, align_bytes=64)
             nc.sync.dma_start(out=w_g[:], in_=ww[:, g, :])
             w_whole.append(w_g)
+        w_a = []
+        for g in range(WHOLE_GROUPS, GROUPS):
+            w_g = keep.tile([P, A_COLS], I32, name="wa%d" % g, align_bytes=64)
+            nc.sync.dma_start(out=w_g[:], in_=ww[:, g, 0:A_COLS])
+            w_a.append(w_g)
+        w_b = []
+        for g in range(WHOLE_GROUPS, LATE_FROM):
+            w_g = keep.tile([P, OUT - A_COLS], I32, name="wb%d" % g, align_bytes=64)
+            nc.sync.dma_start(out=w_g[:], in_=ww[:, g, A_COLS:OUT])
+            w_b.append(w_g)
         w_late = []
-        for t in range(BANKS):
+        for t in range(A_BANKS, BANKS):
             cols = slice(N_TILE * t, N_TILE * (t + 1))
-            w_t = keep.tile([P, GROUPS - WHOLE_GROUPS, N_TILE], I32, name="wl%d" % t, align_bytes=64)
+            w_t = keep.tile([P, GROUPS - LATE_FROM, N_TILE], I32, name="wl%d" % t, align_bytes=64)
             if t < BANKS - 1:
-                nc.sync.dma_start(out=w_t[:], in_=ww[:, WHOLE_GROUPS:GROUPS, cols])
+                nc.sync.dma_start(out=w_t[:], in_=ww[:, LATE_FROM:GROUPS, cols])
             else:
-                for gi in range(GROUPS - WHOLE_GROUPS):
-                    nc.sync.dma_start(out=w_t[:, gi, :], in_=ww[:, WHOLE_GROUPS + gi, cols])
+                for gi in range(GROUPS - LATE_FROM):
+                    nc.sync.dma_start(out=w_t[:, gi, :], in_=ww[:, LATE_FROM + gi, cols])
             w_late.append(w_t)
 
         x_words = x_sb[:].bitcast(F32)
@@ -136,49 +149,64 @@ def tile_modelnew_w_kernel(tc, x, weight_words, weight_scales, bias, out):
         for h in range(2):
             nc.scalar.copy(out=bias_all[:, 512 * h : 512 * (h + 1)], in_=bts[h][:].rearrange("p c n -> p (c n)"))
 
-        def mx_pass(acc, g, t, rhs):
-            k = 4 * (g % 4)
-            nc.tensor.matmul_mx(
-                out=acc[:],
-                lhsT=x_codes[:, B * g : B * (g + 1)].bitcast(FP8X4),
-                lhsT_scale=x_scales[:, B * g : B * (g + 1)],
-                rhs=rhs.bitcast(FP8X4),
-                rhs_scale=planes[g // 4][k:P, N_TILE * t : N_TILE * (t + 1)],
-                start=(g == 0),
-                stop=(g == GROUPS - 1),
-            )
+        def rhs_of(g, t):
+            if g < WHOLE_GROUPS:
+                return w_whole[g][:, N_TILE * t : N_TILE * (t + 1)]
+            if t < A_BANKS:
+                return w_a[g - WHOLE_GROUPS][:, N_TILE * t : N_TILE * (t + 1)]
+            if g < LATE_FROM:
+                return w_b[g - WHOLE_GROUPS][:, N_TILE * (t - A_BANKS) : N_TILE * (t - A_BANKS + 1)]
+            return w_late[t - A_BANKS][:, g - LATE_FROM, :]
 
         accs = []
         for t in range(BANKS):
             acc = psum.tile([P, N_TILE], F32, name="acc%d" % t, tag="bank%d" % t)
             accs.append(acc)
-        for g in range(WHOLE_GROUPS - 1):
-            for t in range(BANKS):
-                mx_pass(accs[t], g, t, w_whole[g][:, N_TILE * t : N_TILE * (t + 1)])
+
+        def mx_pass(g, t):
+            k = 4 * (g % 4)
+            nc.tensor.matmul_mx(
+                out=accs[t][:],
+                lhsT=x_codes[:, B * g : B * (g + 1)].bitcast(FP8X4),
+                lhsT_scale=x_scales[:, B * g : B * (g + 1)],
+                rhs=rhs_of(g, t).bitcast(FP8X4),
+                rhs_scale=planes[g // 4][k:P, N_TILE * t : N_TILE * (t + 1)],
+                start=(g == 0),
+                stop=(g == GROUPS - 1),
+            )
+
+        for g in range(GROUPS):
+            for t in range(BANKS if g < WHOLE_GROUPS else A_BANKS):
+                mx_pass(g, t)
+        for g in range(WHOLE_GROUPS, LATE_FROM):
+            for t in range(A_BANKS, BANKS):
+                mx_pass(g, t)
 
         last = keep.tile([P, J_TILE + 8], F32, name="last")
         gelus = keep.tile([P, BANKS - 1, J_TILE], F32, name="gelus")
+        MAXES = 3
 
-        def bank_max(t0, t1):
+        def bank_max(slot, t0, t1):
             nc.vector.tensor_reduce(
-                out=last[:, J_TILE + t0 : J_TILE + t0 + 1],
+                out=last[:, J_TILE + slot : J_TILE + slot + 1],
                 in_=gelus[:, t0:t1, :].rearrange("p t j -> p (t j)"),
                 axis=AXIS_X,
                 op=MAX,
             )
 
         for t in range(BANKS):
-            g = WHOLE_GROUPS - 1
-            mx_pass(accs[t], g, t, w_whole[g][:, N_TILE * t : N_TILE * (t + 1)])
-            for gi in range(GROUPS - WHOLE_GROUPS):
-                mx_pass(accs[t], WHOLE_GROUPS + gi, t, w_late[t][:, gi, :])
+            if t >= A_BANKS:
+                for g in range(LATE_FROM, GROUPS):
+                    mx_pass(g, t)
             pooled = keep.tile([P, J_TILE], F32, name="pooled%d" % t)
             nc.vector.tensor_reduce(
                 out=pooled[:], in_=accs[t][:].rearrange("p (j i) -> p j i", i=POOL_K), axis=AXIS_X, op=ADD
             )
             biased = keep.tile([P, J_TILE], F32, name="biased%d" % t)
-            if 2 <= t < BANKS - 1:
-                bank_max(t - 2, t - 1)
+            if t == A_BANKS - 1:
+                bank_max(0, 0, A_BANKS - 2)
+            if t == A_BANKS:
+                bank_max(1, A_BANKS - 2, A_BANKS)
             adder = nc.gpsimd if t < BANKS - 1 else nc.vector
             adder.tensor_tensor(
                 out=biased[:], in0=pooled[:], in1=bias_all[:, J_TILE * t : J_TILE * (t + 1)], op=ADD
@@ -187,12 +215,12 @@ def tile_modelnew_w_kernel(tc, x, weight_words, weight_scales, bias, out):
                 nc.scalar.activation(out=gelus[:, t, :], in_=biased[:], func=GELU, scale=1.0 / POOL_K)
             else:
                 nc.scalar.activation(out=last[:, 0:J_TILE], in_=biased[:], func=GELU, scale=1.0 / POOL_K)
-                bank_max(BANKS - 3, BANKS - 1)
+                bank_max(2, A_BANKS, BANKS - 1)
 
         doubled = keep.tile([P, J_TILE + 8], F32, name="doubled")
         nc.vector.tensor_scalar(
-            out=doubled[:, 0 : J_TILE + BANKS - 2],
-            in0=last[:, 0 : J_TILE + BANKS - 2],
+            out=doubled[:, 0 : J_TILE + MAXES],
+            in0=last[:, 0 : J_TILE + MAXES],
             scalar1=2.0,
             scalar2=None,
             op0=MULT,

@@ -28,6 +28,7 @@ J_TILE = N_TILE // POOL_K
 WHOLE_GROUPS = 2
 A_BANKS = 6
 A_COLS = A_BANKS * N_TILE
+ROW_ALIGN = 256
 LATE_FROM = 6
 
 FLOPS = 2 * B * IN * OUT
@@ -42,14 +43,14 @@ def tile_modelnew_w_kernel(tc, x, weight_words, weight_scales, bias, out):
 
         ww = weight_words.bitcast(I32).rearrange("g p n o -> p g (n o)")
 
-        x_sb = keep.tile([P, IN], BF16, name="x_sb")
+        x_sb = keep.tile([P, IN], BF16, name="x_sb", align_bytes=ROW_ALIGN)
         nc.sync.dma_start(out=x_sb[:], in_=x)
         bias_rows = keep.tile([P, N_TILE], BF16, name="bias_rows")
         nc.scalar.dma_start(out=bias_rows[0:BANKS, :], in_=bias.rearrange("(t n) -> t n", t=BANKS))
 
         planes = []
         for h in range(2):
-            plane = keep.tile([P, OUT], U8, name="planes%d" % h, align_bytes=64)
+            plane = keep.tile([P, OUT], U8, name="planes%d" % h, align_bytes=ROW_ALIGN)
             nc.vector.memset(plane[:].bitcast(I32), 0)
             planes.append(plane)
         best = keep.tile([P, 32], F32, name="best", align_bytes=64)
@@ -72,23 +73,23 @@ def tile_modelnew_w_kernel(tc, x, weight_words, weight_scales, bias, out):
 
         w_whole = []
         for g in range(WHOLE_GROUPS):
-            w_g = keep.tile([P, OUT], I32, name="w%d" % g, align_bytes=64)
+            w_g = keep.tile([P, OUT], I32, name="w%d" % g, align_bytes=ROW_ALIGN)
             nc.sync.dma_start(out=w_g[:], in_=ww[:, g, :])
             w_whole.append(w_g)
         w_a = []
         for g in range(WHOLE_GROUPS, GROUPS):
-            w_g = keep.tile([P, A_COLS], I32, name="wa%d" % g, align_bytes=64)
+            w_g = keep.tile([P, A_COLS], I32, name="wa%d" % g, align_bytes=ROW_ALIGN)
             nc.sync.dma_start(out=w_g[:], in_=ww[:, g, 0:A_COLS])
             w_a.append(w_g)
         w_b = []
         for g in range(WHOLE_GROUPS, LATE_FROM):
-            w_g = keep.tile([P, OUT - A_COLS], I32, name="wb%d" % g, align_bytes=64)
+            w_g = keep.tile([P, OUT - A_COLS], I32, name="wb%d" % g, align_bytes=ROW_ALIGN)
             nc.sync.dma_start(out=w_g[:], in_=ww[:, g, A_COLS:OUT])
             w_b.append(w_g)
         w_late = []
         for t in range(A_BANKS, BANKS):
             cols = slice(N_TILE * t, N_TILE * (t + 1))
-            w_t = keep.tile([P, GROUPS - LATE_FROM, N_TILE], I32, name="wl%d" % t, align_bytes=64)
+            w_t = keep.tile([P, GROUPS - LATE_FROM, N_TILE], I32, name="wl%d" % t, align_bytes=ROW_ALIGN)
             if t < BANKS - 1:
                 nc.sync.dma_start(out=w_t[:], in_=ww[:, LATE_FROM:GROUPS, cols])
             else:

@@ -204,16 +204,15 @@ def tile_modelnew_w_kernel(tc, x, weight_words, weight_scales, bias, out):
                 out=pooled[:], in_=accs[t][:].rearrange("p (j i) -> p j i", i=POOL_K), axis=AXIS_X, op=ADD
             )
             biased = keep.tile([P, J_TILE], F32, name="biased%d" % t)
-            if t == A_BANKS - 1:
-                bank_max(0, 0, A_BANKS - 2)
-            if t == A_BANKS:
-                bank_max(1, A_BANKS - 2, A_BANKS)
-            adder = nc.gpsimd if t < BANKS - 1 else nc.vector
+            adder = nc.gpsimd if t < A_BANKS else nc.vector
             adder.tensor_tensor(
                 out=biased[:], in0=pooled[:], in1=bias_all[:, J_TILE * t : J_TILE * (t + 1)], op=ADD
             )
             if t < BANKS - 1:
                 nc.scalar.activation(out=gelus[:, t, :], in_=biased[:], func=GELU, scale=1.0 / POOL_K)
+                if t == A_BANKS - 1:
+                    bank_max(0, 0, A_BANKS - 2)
+                    bank_max(1, A_BANKS - 2, A_BANKS)
             else:
                 nc.scalar.activation(out=last[:, 0:J_TILE], in_=biased[:], func=GELU, scale=1.0 / POOL_K)
                 bank_max(2, A_BANKS, BANKS - 1)

@@ -28,6 +28,7 @@ J_TILE = N_TILE // POOL_K
 WHOLE_GROUPS = 2
 A_BANKS = 6
 A_COLS = A_BANKS * N_TILE
+LAST_A_STEP = 2 * N_TILE
 ROW_ALIGN = 256
 LATE_FROM = 6
 
@@ -79,7 +80,9 @@ def tile_modelnew_w_kernel(tc, x, weight_words, weight_scales, bias, out):
         w_a = []
         for g in range(WHOLE_GROUPS, GROUPS):
             w_g = keep.tile([P, A_COLS], I32, name="wa%d" % g, align_bytes=ROW_ALIGN)
-            nc.sync.dma_start(out=w_g[:], in_=ww[:, g, 0:A_COLS])
+            step = A_COLS if g < GROUPS - 1 else LAST_A_STEP
+            for c0 in range(0, A_COLS, step):
+                nc.sync.dma_start(out=w_g[:, c0 : c0 + step], in_=ww[:, g, c0 : c0 + step])
             w_a.append(w_g)
         w_b = []
         for g in range(WHOLE_GROUPS, LATE_FROM):

@@ -30,6 +30,7 @@ A_BANKS = 6
 A_COLS = A_BANKS * N_TILE
 LAST_A_STEP = 2 * N_TILE
 ROW_ALIGN = 256
+BIAS_AFTER_GROUP = 1
 LATE_FROM = 6
 
 FLOPS = 2 * B * IN * OUT
@@ -122,19 +123,6 @@ def tile_modelnew_w_kernel(tc, x, weight_words, weight_scales, bias, out):
             axis=AXIS_X,
             op=ADD,
         )
-        bts = []
-        for h in range(2):
-            bt = psum.tile([P, 4, P], F32, name="bt%d" % h, tag="bank%d" % (4 + h))
-            for c in range(4):
-                nc.tensor.matmul(
-                    out=bt[:, c, :],
-                    lhsT=ident[:, 4 * h + c : 4 * h + c + 1].to_broadcast([P, P]),
-                    rhs=bias_pool[:],
-                    start=True,
-                    stop=True,
-                )
-            bts.append(bt)
-
         for i in (0, 2):
             nc.vector.tensor_copy(
                 out=grouped_words[:, 2 * i : 2 * i + 2, :, :], in_=xts[i][:].rearrange("p g u b -> p g b u")
@@ -149,10 +137,6 @@ def tile_modelnew_w_kernel(tc, x, weight_words, weight_scales, bias, out):
                 scales=x_scales[:, 512 * half : 512 * (half + 1)],
                 in_=grouped[:, 2048 * half : 2048 * (half + 1)],
             )
-        bias_all = keep.tile([P, OUT // POOL_K], F32, name="bias_all")
-        for h in range(2):
-            nc.scalar.copy(out=bias_all[:, 512 * h : 512 * (h + 1)], in_=bts[h][:].rearrange("p c n -> p (c n)"))
-
         def rhs_of(g, t):
             if g < WHOLE_GROUPS:
                 return w_whole[g][:, N_TILE * t : N_TILE * (t + 1)]
@@ -163,7 +147,7 @@ def tile_modelnew_w_kernel(tc, x, weight_words, weight_scales, bias, out):
             return w_late[t - A_BANKS][:, g - LATE_FROM, :]
 
         accs = []
-        for t in range(BANKS):
+        for t in range(A_BANKS):
             acc = psum.tile([P, N_TILE], F32, name="acc%d" % t, tag="bank%d" % t)
             accs.append(acc)
 
@@ -180,8 +164,31 @@ def tile_modelnew_w_kernel(tc, x, weight_words, weight_scales, bias, out):
             )
 
         for g in range(GROUPS):
-            for t in range(BANKS if g < WHOLE_GROUPS else A_BANKS):
+            for t in range(A_BANKS):
                 mx_pass(g, t)
+            if g == BIAS_AFTER_GROUP:
+                bts = []
+                for h in range(2):
+                    bt = psum.tile([P, 4, P], F32, name="bt%d" % h, tag="bank%d" % (A_BANKS + h))
+                    for c in range(4):
+                        nc.tensor.matmul(
+                            out=bt[:, c, :],
+                            lhsT=ident[:, 4 * h + c : 4 * h + c + 1].to_broadcast([P, P]),
+                            rhs=bias_pool[:],
+                            start=True,
+                            stop=True,
+                        )
+                    bts.append(bt)
+                bias_all = keep.tile([P, OUT // POOL_K], F32, name="bias_all")
+                for h in range(2):
+                    nc.scalar.copy(out=bias_all[:, 512 * h : 512 * (h + 1)], in_=bts[h][:].rearrange("p c n -> p (c n)"))
+                for t in range(A_BANKS, BANKS):
+                    acc = psum.tile([P, N_TILE], F32, name="acc%d" % t, tag="bank%d" % t)
+                    accs.append(acc)
+            if g == BIAS_AFTER_GROUP + 1:
+                for g0 in range(WHOLE_GROUPS):
+                    for t in range(A_BANKS, BANKS):
+                        mx_pass(g0, t)
         for g in range(WHOLE_GROUPS, LATE_FROM):
             for t in range(A_BANKS, BANKS):
                 mx_pass(g, t)

@@ -214,7 +214,7 @@ def tile_modelnew_w_kernel(tc, x, weight_words, weight_scales, bias, out):
                 out=pooled[:], in_=accs[t][:].rearrange("p (j i) -> p j i", i=POOL_K), axis=AXIS_X, op=ADD
             )
             biased = keep.tile([P, J_TILE], F32, name="biased%d" % t)
-            adder = nc.gpsimd if t < A_BANKS else nc.vector
+            adder = nc.gpsimd if t < BANKS - 1 else nc.vector
             adder.tensor_tensor(
                 out=biased[:], in0=pooled[:], in1=bias_all[:, J_TILE * t : J_TILE * (t + 1)], op=ADD
             )

from contextlib import ExitStack

import concourse.mybir as mybir
from concourse.masks import make_identity

F32 = mybir.dt.float32
BF16 = mybir.dt.bfloat16
I32 = mybir.dt.int32
U32 = mybir.dt.uint32
U8 = mybir.dt.uint8
FP8X4 = mybir.dt.float8_e4m3fn_x4
ADD = mybir.AluOpType.add
MAX = mybir.AluOpType.max
MULT = mybir.AluOpType.mult
AXIS_X = mybir.AxisListType.X
GELU = mybir.ActivationFunctionType.Gelu_apprx_tanh

P = 128
B = 128
IN = 4096
OUT = 4096
POOL_K = 4
K_PASS = 512
GROUPS = IN // K_PASS
N_TILE = 512
BANKS = OUT // N_TILE
J_TILE = N_TILE // POOL_K
WHOLE_GROUPS = 2
A_BANKS = 6
A_COLS = A_BANKS * N_TILE
LAST_A_STEP = 2 * N_TILE
ROW_ALIGN = 256
BIAS_AFTER_GROUP = 1
LATE_FROM = 6

FLOPS = 2 * B * IN * OUT


def tile_modelnew_w_kernel(tc, x, weight_words, weight_scales, bias, out):
    nc = tc.nc
    with ExitStack() as ctx:
        ctx.enter_context(tc.manual_schedule())
        keep = ctx.enter_context(tc.tile_pool(name="keep", bufs=1))
        psum = ctx.enter_context(tc.psum_pool(name="psum", bufs=1))

        ww = weight_words.bitcast(I32).rearrange("g p n o -> p g (n o)")

        x_sb = keep.tile([P, IN], BF16, name="x_sb", align_bytes=ROW_ALIGN)
        nc.sync.dma_start(out=x_sb[:], in_=x)
        bias_rows = keep.tile([P, N_TILE], BF16, name="bias_rows")
        nc.scalar.dma_start(out=bias_rows[0:BANKS, :], in_=bias.rearrange("(t n) -> t n", t=BANKS))

        planes = []
        for h in range(2):
            plane = keep.tile([P, OUT], U8, name="planes%d" % h, align_bytes=ROW_ALIGN)
            nc.vector.memset(plane[:].bitcast(I32), 0)
            planes.append(plane)
        best = keep.tile([P, 32], F32, name="best", align_bytes=64)
        nc.vector.memset(best[:], 0.0)
        warm = keep.tile([P, 1], F32, name="warm")
        nc.vector.memset(warm[:], 0.0)
        warm_out = keep.tile([P, 1], F32, name="warm_out")
        nc.scalar.activation(out=warm_out[:], in_=warm[:], func=GELU)

        ident = keep.tile([P, P], F32, name="ident")
        make_identity(nc, ident[:])

        for h in range(2):
            for q in range(4):
                queue, view = (nc.sync, I32) if q < 2 else (nc.gpsimd, F32)
                queue.dma_start(
                    out=planes[h][32 * q : 32 * q + 16, :].bitcast(view),
                    in_=weight_scales[4 * h : 4 * h + 4, 4 * q : 4 * q + 4, :].bitcast(view),
                )

        w_whole = []
        for g in range(WHOLE_GROUPS):
            w_g = keep.tile([P, OUT], I32, name="w%d" % g, align_bytes=ROW_ALIGN)
            nc.sync.dma_start(out=w_g[:], in_=ww[:, g, :])
            w_whole.append(w_g)
        w_a = []
        for g in range(WHOLE_GROUPS, GROUPS):
            w_g = keep.tile([P, A_COLS], I32, name="wa%d" % g, align_bytes=ROW_ALIGN)
            step = A_COLS if g < GROUPS - 1 else LAST_A_STEP
            for c0 in range(0, A_COLS, step):
                nc.sync.dma_start(out=w_g[:, c0 : c0 + step], in_=ww[:, g, c0 : c0 + step])
            w_a.append(w_g)
        w_b = []
        for g in range(WHOLE_GROUPS, LATE_FROM):
            w_g = keep.tile([P, OUT - A_COLS], I32, name="wb%d" % g, align_bytes=ROW_ALIGN)
            nc.sync.dma_start(out=w_g[:], in_=ww[:, g, A_COLS:OUT])
            w_b.append(w_g)
        w_late = []
        for t in range(A_BANKS, BANKS):
            cols = slice(N_TILE * t, N_TILE * (t + 1))
            w_t = keep.tile([P, GROUPS - LATE_FROM, N_TILE], I32, name="wl%d" % t, align_bytes=ROW_ALIGN)
            if t < BANKS - 1:
                nc.sync.dma_start(out=w_t[:], in_=ww[:, LATE_FROM:GROUPS, cols])
            else:
                for gi in range(GROUPS - LATE_FROM):
                    nc.sync.dma_start(out=w_t[:, gi, :], in_=ww[:, LATE_FROM + gi, cols])
            w_late.append(w_t)

        x_words = x_sb[:].bitcast(F32)
        grouped = keep.tile([P, IN], BF16, name="grouped", align_bytes=64)
        grouped_words = grouped[:].bitcast(F32).rearrange("p (g b u) -> p g b u", g=GROUPS, u=2)
        x_codes = keep.tile([P, GROUPS * B], U32, name="x_codes", align_bytes=64)
        x_scales = keep.tile([P, GROUPS * B], U8, name="x_scales", align_bytes=64)
        xts = []
        for i in range(4):
            xt = psum.tile([P, 2, 2, B], F32, name="xt%d" % i, tag="bank%d" % i)
            for gl in range(2):
                g = 2 * i + gl
                for u in range(2):
                    nc.tensor.transpose(xt[:, gl, u, :], x_words[:, 256 * g + u : 256 * (g + 1) : 2], ident[:])
            xts.append(xt)

        bias_pool = keep.tile([P, J_TILE], F32, name="bias_pool")
        nc.vector.memset(bias_pool[:], 0.0)
        nc.vector.tensor_reduce(
            out=bias_pool[0:BANKS, :],
            in_=bias_rows[0:BANKS, :].rearrange("p (j i) -> p j i", i=POOL_K),
            axis=AXIS_X,
            op=ADD,
        )
        for i in (0, 2):
            nc.vector.tensor_copy(
                out=grouped_words[:, 2 * i : 2 * i + 2, :, :], in_=xts[i][:].rearrange("p g u b -> p g b u")
            )
            nc.scalar.copy(
                out=grouped_words[:, 2 * i + 2 : 2 * i + 4, :, :],
                in_=xts[i + 1][:].rearrange("p g u b -> p g b u"),
            )
        for half in range(2):
            nc.vector.quantize_mx(
                out=x_codes[:, 512 * half : 512 * (half + 1)].bitcast(FP8X4),
                scales=x_scales[:, 512 * half : 512 * (half + 1)],
                in_=grouped[:, 2048 * half : 2048 * (half + 1)],
            )
        def rhs_of(g, t):
            if g < WHOLE_GROUPS:
                return w_whole[g][:, N_TILE * t : N_TILE * (t + 1)]
            if t < A_BANKS:
                return w_a[g - WHOLE_GROUPS][:, N_TILE * t : N_TILE * (t + 1)]
            if g < LATE_FROM:
                return w_b[g - WHOLE_GROUPS][:, N_TILE * (t - A_BANKS) : N_TILE * (t - A_BANKS + 1)]
            return w_late[t - A_BANKS][:, g - LATE_FROM, :]

        accs = []
        for t in range(A_BANKS):
            acc = psum.tile([P, N_TILE], F32, name="acc%d" % t, tag="bank%d" % t)
            accs.append(acc)

        def mx_pass(g, t):
            k = 4 * (g % 4)
            nc.tensor.matmul_mx(
                out=accs[t][:],
                lhsT=x_codes[:, B * g : B * (g + 1)].bitcast(FP8X4),
                lhsT_scale=x_scales[:, B * g : B * (g + 1)],
                rhs=rhs_of(g, t).bitcast(FP8X4),
                rhs_scale=planes[g // 4][k:P, N_TILE * t : N_TILE * (t + 1)],
                start=(g == 0),
                stop=(g == GROUPS - 1),
            )

        for g in range(GROUPS):
            for t in range(A_BANKS):
                mx_pass(g, t)
            if g == BIAS_AFTER_GROUP:
                bts = []
                for h in range(2):
                    bt = psum.tile([P, 4, P], F32, name="bt%d" % h, tag="bank%d" % (A_BANKS + h))
                    for c in range(4):
                        nc.tensor.matmul(
                            out=bt[:, c, :],
                            lhsT=ident[:, 4 * h + c : 4 * h + c + 1].to_broadcast([P, P]),
                            rhs=bias_pool[:],
                            start=True,
                            stop=True,
                        )
                    bts.append(bt)
                bias_all = keep.tile([P, OUT // POOL_K], F32, name="bias_all")
                for h in range(2):
                    nc.scalar.copy(out=bias_all[:, 512 * h : 512 * (h + 1)], in_=bts[h][:].rearrange("p c n -> p (c n)"))
                for t in range(A_BANKS, BANKS):
                    acc = psum.tile([P, N_TILE], F32, name="acc%d" % t, tag="bank%d" % t)
                    accs.append(acc)
            if g == BIAS_AFTER_GROUP + 1:
                for g0 in range(WHOLE_GROUPS):
                    for t in range(A_BANKS, BANKS):
                        mx_pass(g0, t)
        for g in range(WHOLE_GROUPS, LATE_FROM):
            for t in range(A_BANKS, BANKS):
                mx_pass(g, t)

        last = keep.tile([P, J_TILE + 8], F32, name="last")
        gelus = keep.tile([P, BANKS - 1, J_TILE], F32, name="gelus")
        MAXES = 3

        def bank_max(slot, t0, t1):
            nc.vector.tensor_reduce(
                out=last[:, J_TILE + slot : J_TILE + slot + 1],
                in_=gelus[:, t0:t1, :].rearrange("p t j -> p (t j)"),
                axis=AXIS_X,
                op=MAX,
            )

        for t in range(BANKS):
            if t >= A_BANKS:
                for g in range(LATE_FROM, GROUPS):
                    mx_pass(g, t)
            pooled = keep.tile([P, J_TILE], F32, name="pooled%d" % t)
            nc.vector.tensor_reduce(
                out=pooled[:], in_=accs[t][:].rearrange("p (j i) -> p j i", i=POOL_K), axis=AXIS_X, op=ADD
            )
            biased = keep.tile([P, J_TILE], F32, name="biased%d" % t)
            adder = nc.gpsimd if t < BANKS - 1 else nc.vector
            adder.tensor_tensor(
                out=biased[:], in0=pooled[:], in1=bias_all[:, J_TILE * t : J_TILE * (t + 1)], op=ADD
            )
            if t < BANKS - 1:
                nc.scalar.activation(out=gelus[:, t, :], in_=biased[:], func=GELU, scale=1.0 / POOL_K)
                if t == A_BANKS - 1:
                    bank_max(0, 0, A_BANKS - 2)
                    bank_max(1, A_BANKS - 2, A_BANKS)
            else:
                nc.scalar.activation(out=last[:, 0:J_TILE], in_=biased[:], func=GELU, scale=1.0 / POOL_K)
                bank_max(2, A_BANKS, BANKS - 1)

        doubled = keep.tile([P, J_TILE + 8], F32, name="doubled")
        nc.vector.tensor_scalar(
            out=doubled[:, 0 : J_TILE + MAXES],
            in0=last[:, 0 : J_TILE + MAXES],
            scalar1=2.0,
            scalar2=None,
            op0=MULT,
            op1=MAX,
            accum_out=best[:, 0:1],
        )
        rows = keep.tile([P, 32], F32, name="rows", align_bytes=64)
        nc.vector.transpose(out=rows[:], in_=best[:])
        nc.sync.dma_start(out=out.rearrange("(q b) -> q b", q=4), in_=rows[0:P:32, :])
